import numpy as np
import ml_dtypes


def mxq(x, axis, fmt="e4m3"):
    dtype, down = {"e4m3": (ml_dtypes.float8_e4m3fn, 7), "e5m2": (ml_dtypes.float8_e5m2, 14)}[fmt]
    v = np.moveaxis(np.asarray(x, np.float32).astype(ml_dtypes.bfloat16).astype(np.float64), axis, -1)
    blocks = v.reshape(v.shape[:-1] + (-1, 32))
    amax = np.abs(blocks).max(-1, keepdims=True)
    byte = np.maximum(np.where(amax > 0, np.frexp(amax)[1] - 1 + 127, 0) - down, 1)
    scale = np.exp2(byte - 127.0)
    codes = (blocks / scale).astype(np.float32).astype(dtype).astype(np.float64)
    return np.moveaxis((codes * scale).reshape(v.shape), -1, axis)


WIDE = False


def mx_kscale(k):
    if not WIDE:
        return np.ones(k)
    levels = np.array([10, -10, 5, -5, 0])
    a = np.random.permutation(np.resize(levels, k // 512 * 4)).reshape(k // 512, 4)
    idx = np.arange(k)
    return np.exp2(a[idx // 512, idx % 128 // 32])


BF16 = ml_dtypes.bfloat16


def bf(x):
    return np.asarray(x, np.float32).astype(BF16)


def f64(x):
    return np.asarray(x).astype(np.float64)


E2M1 = np.array([0.0, 0.5, 1.0, 1.5, 2.0, 3.0, 4.0, 6.0, -0.0, -0.5, -1.0, -1.5, -2.0, -3.0, -4.0, -6.0])


def pack_weight(w, fmt):
    k, n = w.shape
    w = f64(bf(w)).reshape(k // 32, 32, n)
    amax = np.abs(w).max(1)
    if fmt == "e4m3":
        byte = np.frexp(amax)[1] - 1 + 127 - 7
    else:
        mant, ex = np.frexp(amax / 6.0)
        byte = np.where(mant > 0.5, ex, ex - 1) + 127
    byte = np.clip(np.where(amax > 0, byte, 1), 1, 254)
    scaled = (w * np.exp2(127.0 - byte)[:, None, :]).reshape(k, n).astype(np.float32)
    by_word = np.ascontiguousarray(scaled.reshape(k // 512, 128, 4, n).transpose(0, 1, 3, 2))
    if fmt == "e4m3":
        words = by_word.astype(ml_dtypes.float8_e4m3fn).view(np.uint8)
    else:
        c = by_word.astype(ml_dtypes.float4_e2m1fn).view(np.uint8) & 0xF
        words = c[..., 0::2] | (c[..., 1::2] << 4)
    return np.ascontiguousarray(words), np.ascontiguousarray(byte.astype(np.uint8).reshape(k // 512, 16, n))


def unpack_weight(words, scales, fmt):
    g, p, n, _ = words.shape
    if fmt == "e4m3":
        vals = np.ascontiguousarray(words).view(ml_dtypes.float8_e4m3fn).astype(np.float64)
    else:
        nib = np.empty((g, p, n, 4), np.uint8)
        nib[..., 0::2] = words & 0xF
        nib[..., 1::2] = words >> 4
        vals = E2M1[nib]
    vals = vals * np.repeat(np.exp2(scales.astype(np.float64) - 127.0), 8, axis=1)[..., None]
    return vals.transpose(0, 1, 3, 2).reshape(g * 512, n)

def pack4(w):
    words, scales = pack_weight(w, "e2m1")
    return words.reshape(words.shape[0], 128, -1), scales


def unpack4(words, scales):
    return unpack_weight(words.reshape(words.shape[0], 128, -1, 2), scales, "e2m1")


B, IDIM, HDIM, ODIM, S, DEPTH, NACT, NTOP = 4096, 1024, 512, 512, 128, 32, 3, 2


def sigmoid(v):
    return 1.0 / (1.0 + np.exp(-v))


def setup_inputs():
    s, t = mx_kscale(IDIM), mx_kscale(HDIM)
    x = bf(np.random.standard_normal((B, IDIM)) * s)
    hidden = bf(np.random.standard_normal((B, HDIM)) * t)
    stack_top = bf(np.random.standard_normal((B, NTOP, S)))
    Wi = np.random.standard_normal((HDIM, IDIM)) * 0.7 / np.sqrt(IDIM) / s
    bi = bf(np.random.standard_normal(HDIM) * 0.2)
    Wh = np.random.standard_normal((HDIM, HDIM)) * 0.7 / np.sqrt(HDIM) / t
    bh = bf(np.random.standard_normal(HDIM) * 0.2)
    W0 = bf(np.random.standard_normal((HDIM, S)) * 0.5 / np.sqrt(S))
    b0 = bf(np.random.standard_normal(HDIM) * 0.2)
    W1 = bf(np.random.standard_normal((HDIM, S)) * 0.5 / np.sqrt(S))
    b1 = bf(np.random.standard_normal(HDIM) * 0.2)
    Wi_words, Wi_scales = pack4(np.ascontiguousarray(Wi.T))
    Wh_words, Wh_scales = pack4(np.ascontiguousarray(Wh.T))
    return {"x": x,
            "hidden": hidden,
            "stack_top": stack_top,
            "Wi_words": Wi_words,
            "Wi_scales": Wi_scales,
            "bi": bi,
            "Wh_words": Wh_words,
            "Wh_scales": Wh_scales,
            "bh": bh,
            "W0": W0,
            "b0": b0,
            "W1": W1,
            "b1": b1}


def reference(x, hidden, stack_top, Wi_words, Wi_scales, bi, Wh_words, Wh_scales, bh, W0, b0, W1, b1):
    pre = ((mxq(f64(x), 1, "e4m3") @ unpack4(Wi_words, Wi_scales)) + f64(bi)
           + (mxq(f64(hidden), 1, "e4m3") @ unpack4(Wh_words, Wh_scales)) + f64(bh)
           + f64(stack_top)[:, 0] @ f64(W0).T + f64(b0)
           + f64(stack_top)[:, 1] @ f64(W1).T + f64(b1))
    return sigmoid(pre)

@@ -1,0 +1,229 @@
+from contextlib import ExitStack
+
+import concourse.mybir as mybir
+from concourse.masks import make_identity
+
+F32 = mybir.dt.float32
+BF16 = mybir.dt.bfloat16
+I32 = mybir.dt.int32
+U32 = mybir.dt.uint32
+U8 = mybir.dt.uint8
+FP8X4 = mybir.dt.float8_e4m3fn_x4
+FP4X4 = mybir.dt.float4_e2m1fn_x4
+ADD = mybir.AluOpType.add
+SIGMOID = mybir.ActivationFunctionType.Sigmoid
+
+P = 128
+PACK = 4
+K_PASS = P * PACK
+HALVES = 2
+
+BATCH, IDIM, HDIM, STACK = 4096, 1024, 512, 256
+X_PASSES = IDIM // K_PASS
+H_PASSES = HDIM // K_PASS
+W_PASSES = X_PASSES + H_PASSES
+TILES = BATCH // P
+GROUP_TILES = 2
+GROUPS = TILES // GROUP_TILES
+OUT_BLOCKS = HDIM // P
+
+FLOPS = 2 * BATCH * HDIM * (IDIM + HDIM + STACK)
+
+
+def tile_stackrnn_pa_t_kernel(
+    tc, x, hidden, stack_top, Wi_words, Wi_scales, bi, Wh_words, Wh_scales, bh, W0, b0, W1, b1, out
+):
+    nc = tc.nc
+    x_tiles = x.rearrange("(p t) k -> p t k", t=TILES)
+    h_tiles = hidden.rearrange("(p t) k -> p t k", t=TILES)
+    s_tiles = stack_top.rearrange("(p t) a s -> p t (a s)", t=TILES)
+    out_tiles = out.rearrange("(p t) n -> p t n", t=TILES)
+
+    with ExitStack() as ctx:
+        ctx.enter_context(tc.manual_schedule())
+        consts = ctx.enter_context(tc.tile_pool(name="consts", bufs=1))
+        inputs = ctx.enter_context(tc.tile_pool(name="inputs", bufs=GROUPS))
+        work = ctx.enter_context(tc.tile_pool(name="work", bufs=2))
+        results = ctx.enter_context(tc.tile_pool(name="results", bufs=4))
+        psum_one = ctx.enter_context(tc.psum_pool(name="psum_one", bufs=1))
+        psum_two = ctx.enter_context(tc.psum_pool(name="psum_two", bufs=GROUP_TILES))
+
+        w_scales = consts.tile([P, W_PASSES, HDIM], U8, align_bytes=64)
+        nc.vector.memset(w_scales[:].rearrange("p a n -> p (a n)").bitcast(I32), 0)
+        bias_rows = consts.tile([P, HDIM], BF16)
+        nc.vector.memset(bias_rows[:], 0.0)
+        ones = consts.tile([P, P], BF16)
+        nc.vector.memset(ones[:], 1.0)
+        zero_column = consts.tile([P, 1], F32)
+        nc.vector.memset(zero_column[:], 0.0)
+        identity = consts.tile([P, P], F32)
+        make_identity(nc, identity[:])
+
+        x_in, h_in, s_in = [], [], []
+
+        def load_group(g):
+            tiles_of_g = slice(g * GROUP_TILES, (g + 1) * GROUP_TILES)
+            x_g = inputs.tile([P, GROUP_TILES, IDIM], BF16, name="x_g")
+            nc.sync.dma_start(out=x_g[:], in_=x_tiles[:, tiles_of_g, :])
+            h_g = inputs.tile([P, GROUP_TILES, HDIM], BF16, name="h_g")
+            nc.sync.dma_start(out=h_g[:], in_=h_tiles[:, tiles_of_g, :])
+            s_g = inputs.tile([P, GROUP_TILES, STACK], BF16, name="s_g")
+            nc.sync.dma_start(out=s_g[:], in_=s_tiles[:, tiles_of_g, :])
+            x_in.append(x_g)
+            h_in.append(h_g)
+            s_in.append(s_g)
+
+        load_group(0)
+
+        w_words = consts.tile([P, W_PASSES, 2 * HDIM], U8, align_bytes=64)
+        nc.sync.dma_start(
+            out=w_words[:, 0:X_PASSES, :].bitcast(I32),
+            in_=Wi_words.bitcast(I32).rearrange("g p n -> p g n"),
+        )
+        nc.sync.dma_start(
+            out=w_words[:, X_PASSES:W_PASSES, :].bitcast(I32),
+            in_=Wh_words.bitcast(I32).rearrange("g p n -> p g n"),
+        )
+        for quadrant in range(4):
+            rows = slice(4 * quadrant, 4 * quadrant + 4)
+            parts = slice(32 * quadrant, 32 * quadrant + 4)
+            nc.sync.dma_start(
+                out=w_scales[parts, 0:X_PASSES, :].bitcast(I32),
+                in_=Wi_scales[:, rows, :].bitcast(I32).rearrange("g r n -> r g n"),
+            )
+            nc.sync.dma_start(
+                out=w_scales[parts, X_PASSES:W_PASSES, :].bitcast(I32),
+                in_=Wh_scales[:, rows, :].bitcast(I32).rearrange("g r n -> r g n"),
+            )
+
+        for g in range(1, GROUPS):
+            load_group(g)
+
+        w_cat = consts.tile([P, OUT_BLOCKS, STACK], BF16)
+        nc.scalar.dma_start(out=w_cat[:, :, 0 : STACK // 2], in_=W0.rearrange("(j n) s -> n j s", n=P))
+        nc.scalar.dma_start(out=w_cat[:, :, STACK // 2 : STACK], in_=W1.rearrange("(j n) s -> n j s", n=P))
+        for row, bias in enumerate((bi, bh, b0, b1)):
+            nc.scalar.dma_start(out=bias_rows[row : row + 1, :], in_=bias.rearrange("(o n) -> o n", o=1))
+        nc.scalar.activation(out=zero_column[:], in_=zero_column[:], func=SIGMOID)
+
+        grouped = {}
+        quantised = {}
+        sums = {}
+
+        def transpose_group(g):
+            x_words = x_in[g][:].bitcast(F32)
+            h_words = h_in[g][:].bitcast(F32)
+            s_words = s_in[g][:].bitcast(F32)
+            words_in_pass = K_PASS // 2
+            x_t = []
+            h_t = psum_one.tile([P, GROUP_TILES, HALVES, P], F32, name="h_t")
+            s_t = psum_one.tile([P, GROUP_TILES, P], F32, name="s_t")
+            for r in range(GROUP_TILES):
+                x_t_r = psum_two.tile([P, X_PASSES, HALVES, P], F32, name="x_t_r")
+                for a in range(X_PASSES):
+                    for u in range(HALVES):
+                        every_second = slice(a * words_in_pass + u, (a + 1) * words_in_pass, HALVES)
+                        nc.tensor.transpose(x_t_r[:, a, u, :], x_words[:, r, every_second], identity[:])
+                x_t.append(x_t_r)
+                for u in range(HALVES):
+                    nc.tensor.transpose(h_t[:, r, u, :], h_words[:, r, u:words_in_pass:HALVES], identity[:])
+                nc.tensor.transpose(s_t[:, r, :], s_words[:, r, :], identity[:])
+            return x_t, h_t, s_t
+
+        def copy_out_group(g, x_t, h_t, s_t):
+            x_k = work.tile([P, GROUP_TILES, X_PASSES, P, PACK], BF16, name="x_k", align_bytes=64)
+            h_k = work.tile([P, GROUP_TILES, P, PACK], BF16, name="h_k", align_bytes=64)
+            s_k = work.tile([P, GROUP_TILES, P, 2], BF16, name="s_k")
+            for r in range(GROUP_TILES):
+                nc.scalar.copy(
+                    out=x_k[:, r].rearrange("p a c t -> p a (c t)").bitcast(F32).rearrange("p a (c u) -> p a c u", u=HALVES),
+                    in_=x_t[r][:].rearrange("p a u c -> p a c u"),
+                )
+            nc.scalar.copy(
+                out=h_k[:].rearrange("p r c t -> p r (c t)").bitcast(F32).rearrange("p r (c u) -> p r c u", u=HALVES),
+                in_=h_t[:].rearrange("p r u c -> p r c u"),
+            )
+            nc.scalar.copy(out=s_k[:].rearrange("p r c e -> p r (c e)").bitcast(F32), in_=s_t[:])
+            grouped[g] = (x_k, h_k, s_k)
+
+        def quantise_group(g):
+            x_k, h_k, s_k = grouped[g]
+            x_codes = work.tile([P, GROUP_TILES, X_PASSES, P], U32, name="x_codes", align_bytes=64)
+            x_scales = work.tile([P, GROUP_TILES, X_PASSES, P], U8, name="x_scales", align_bytes=64)
+            nc.vector.quantize_mx(
+                out=x_codes[:].rearrange("p r a c -> p (r a c)").bitcast(FP8X4),
+                scales=x_scales[:].rearrange("p r a c -> p (r a c)"),
+                in_=x_k[:].rearrange("p r a c t -> p (r a c t)"),
+            )
+            h_codes = work.tile([P, GROUP_TILES, P], U32, name="h_codes", align_bytes=64)
+            h_scales = work.tile([P, GROUP_TILES, P], U8, name="h_scales", align_bytes=64)
+            nc.vector.quantize_mx(
+                out=h_codes[:].rearrange("p r c -> p (r c)").bitcast(FP8X4),
+                scales=h_scales[:].rearrange("p r c -> p (r c)"),
+                in_=h_k[:].rearrange("p r c t -> p (r c t)"),
+            )
+            quantised[g] = (x_codes, x_scales, h_codes, h_scales)
+
+        def stack_product_group(g):
+            s_k = grouped[g][2]
+            pre = results.tile([P, GROUP_TILES, HDIM], F32, name="pre")
+            for r in range(GROUP_TILES):
+                stack_ps = psum_two.tile([P, HDIM], F32, name="stack_ps")
+                for e in range(2):
+                    nc.tensor.matmul(
+                        out=stack_ps[:], lhsT=s_k[:, r, :, e], rhs=w_stack[:, e, :], start=(e == 0), stop=(e == 1)
+                    )
+                nc.vector.tensor_tensor(out=pre[:, r, :], in0=stack_ps[:], in1=bias_all[:], op=ADD)
+            sums[g] = [pre]
+
+        def mx_product_group(g):
+            x_codes, x_scales, h_codes, h_scales = quantised[g]
+            for r in range(GROUP_TILES):
+                mx_ps = psum_two.tile([P, HDIM], F32, name="mx_ps")
+                for a in range(W_PASSES):
+                    if a < X_PASSES:
+                        codes, scales = x_codes[:, r, a, :], x_scales[:, r, a, :]
+                    else:
+                        codes, scales = h_codes[:, r, :], h_scales[:, r, :]
+                    nc.tensor.matmul_mx(
+                        out=mx_ps[:],
+                        lhsT=codes.bitcast(FP8X4),
+                        lhsT_scale=scales,
+                        rhs=w_words[:, a, :].bitcast(FP4X4),
+                        rhs_scale=w_scales[:, a, :],
+                        start=(a == 0),
+                        stop=(a == W_PASSES - 1),
+                    )
+                sums[g].append(mx_ps)
+
+        def finish_group(g):
+            pre = sums[g][0]
+            for r in range(GROUP_TILES):
+                nc.vector.tensor_tensor(out=pre[:, r, :], in0=sums[g][1 + r][:], in1=pre[:, r, :], op=ADD)
+                nc.scalar.activation(out=pre[:, r, :], in_=pre[:, r, :], func=SIGMOID)
+            nc.scalar.dma_start(out=out_tiles[:, g * GROUP_TILES : (g + 1) * GROUP_TILES, :], in_=pre[:])
+
+        copy_out_group(0, *transpose_group(0))
+
+        w_cat_t = psum_two.tile([P, OUT_BLOCKS, P], F32, tag="stack_ps")
+        for j in range(OUT_BLOCKS):
+            nc.tensor.transpose(w_cat_t[:, j, :], w_cat[:, j, :].bitcast(F32), identity[:])
+        w_stack = consts.tile([P, 2, HDIM], BF16)
+        nc.vector.tensor_copy(
+            out=w_stack[:],
+            in_=w_cat_t[:].rearrange("p j n -> p (j n)").bitcast(BF16).rearrange("p (n e) -> p e n", e=2),
+        )
+        bias_ps = psum_two.tile([P, HDIM], F32, tag="stack_ps")
+        nc.tensor.matmul(out=bias_ps[:], lhsT=ones[:], rhs=bias_rows[:], start=True, stop=True)
+        bias_all = consts.tile([P, HDIM], F32)
+        nc.vector.tensor_copy(out=bias_all[:], in_=bias_ps[:])
+
+        for g in range(GROUPS):
+            if g + 1 < GROUPS:
+                copy_out_group(g + 1, *transpose_group(g + 1))
+            quantise_group(g)
+            if g > 0:
+                finish_group(g - 1)
+            stack_product_group(g)
+            mx_product_group(g)
+        finish_group(GROUPS - 1)

@@ -44,9 +44,8 @@ def tile_stackrnn_pa_t_kernel(
         consts = ctx.enter_context(tc.tile_pool(name="consts", bufs=1))
         inputs = ctx.enter_context(tc.tile_pool(name="inputs", bufs=GROUPS))
         work = ctx.enter_context(tc.tile_pool(name="work", bufs=2))
-        results = ctx.enter_context(tc.tile_pool(name="results", bufs=4))
-        psum_one = ctx.enter_context(tc.psum_pool(name="psum_one", bufs=1))
-        psum_two = ctx.enter_context(tc.psum_pool(name="psum_two", bufs=GROUP_TILES))
+        results = ctx.enter_context(tc.tile_pool(name="results", bufs=5))
+        psum = ctx.enter_context(tc.psum_pool(name="psum", bufs=GROUP_TILES))
 
         w_scales = consts.tile([P, W_PASSES, HDIM], U8, align_bytes=64)
         nc.vector.memset(w_scales[:].rearrange("p a n -> p (a n)").bitcast(I32), 0)
@@ -106,45 +105,49 @@ def tile_stackrnn_pa_t_kernel(
             nc.scalar.dma_start(out=bias_rows[row : row + 1, :], in_=bias.rearrange("(o n) -> o n", o=1))
         nc.scalar.activation(out=zero_column[:], in_=zero_column[:], func=SIGMOID)
 
+        transposed = {}
         grouped = {}
         quantised = {}
-        sums = {}
+        pre_act = {}
+        mx_sums = {}
+        words_in_pass = K_PASS // 2
 
-        def transpose_group(g):
+        def transpose_x(g, r):
             x_words = x_in[g][:].bitcast(F32)
+            x_t = psum.tile([P, X_PASSES, HALVES, P], F32, name="x_t")
+            for a in range(X_PASSES):
+                for u in range(HALVES):
+                    every_second = slice(a * words_in_pass + u, (a + 1) * words_in_pass, HALVES)
+                    nc.tensor.transpose(x_t[:, a, u, :], x_words[:, r, every_second], identity[:])
+            return x_t
+
+        def transpose_hidden_and_stack(g, r):
             h_words = h_in[g][:].bitcast(F32)
             s_words = s_in[g][:].bitcast(F32)
-            words_in_pass = K_PASS // 2
-            x_t = []
-            h_t = psum_one.tile([P, GROUP_TILES, HALVES, P], F32, name="h_t")
-            s_t = psum_one.tile([P, GROUP_TILES, P], F32, name="s_t")
-            for r in range(GROUP_TILES):
-                x_t_r = psum_two.tile([P, X_PASSES, HALVES, P], F32, name="x_t_r")
-                for a in range(X_PASSES):
-                    for u in range(HALVES):
-                        every_second = slice(a * words_in_pass + u, (a + 1) * words_in_pass, HALVES)
-                        nc.tensor.transpose(x_t_r[:, a, u, :], x_words[:, r, every_second], identity[:])
-                x_t.append(x_t_r)
-                for u in range(HALVES):
-                    nc.tensor.transpose(h_t[:, r, u, :], h_words[:, r, u:words_in_pass:HALVES], identity[:])
-                nc.tensor.transpose(s_t[:, r, :], s_words[:, r, :], identity[:])
-            return x_t, h_t, s_t
+            hs_t = psum.tile([P, HALVES + 1, P], F32, name="hs_t")
+            for u in range(HALVES):
+                nc.tensor.transpose(hs_t[:, u, :], h_words[:, r, u:words_in_pass:HALVES], identity[:])
+            nc.tensor.transpose(hs_t[:, HALVES, :], s_words[:, r, :], identity[:])
+            return hs_t
 
-        def copy_out_group(g, x_t, h_t, s_t):
+        def new_grouped_tiles(g):
             x_k = work.tile([P, GROUP_TILES, X_PASSES, P, PACK], BF16, name="x_k", align_bytes=64)
             h_k = work.tile([P, GROUP_TILES, P, PACK], BF16, name="h_k", align_bytes=64)
             s_k = work.tile([P, GROUP_TILES, P, 2], BF16, name="s_k")
-            for r in range(GROUP_TILES):
-                nc.scalar.copy(
-                    out=x_k[:, r].rearrange("p a c t -> p a (c t)").bitcast(F32).rearrange("p a (c u) -> p a c u", u=HALVES),
-                    in_=x_t[r][:].rearrange("p a u c -> p a c u"),
-                )
-            nc.scalar.copy(
-                out=h_k[:].rearrange("p r c t -> p r (c t)").bitcast(F32).rearrange("p r (c u) -> p r c u", u=HALVES),
-                in_=h_t[:].rearrange("p r u c -> p r c u"),
-            )
-            nc.scalar.copy(out=s_k[:].rearrange("p r c e -> p r (c e)").bitcast(F32), in_=s_t[:])
             grouped[g] = (x_k, h_k, s_k)
+
+        def copy_out_tile(g, r):
+            x_k, h_k, s_k = grouped[g]
+            x_t, hs_t = transposed[(g, r)]
+            nc.scalar.copy(
+                out=x_k[:, r].rearrange("p a c t -> p a (c t)").bitcast(F32).rearrange("p a (c u) -> p a c u", u=HALVES),
+                in_=x_t[:].rearrange("p a u c -> p a c u"),
+            )
+            nc.scalar.copy(
+                out=h_k[:, r].rearrange("p c t -> p (c t)").bitcast(F32).rearrange("p (c u) -> p c u", u=HALVES),
+                in_=hs_t[:, 0:HALVES, :].rearrange("p u c -> p c u"),
+            )
+            nc.scalar.copy(out=s_k[:, r].rearrange("p c e -> p (c e)").bitcast(F32), in_=hs_t[:, HALVES, :])
 
         def quantise_group(g):
             x_k, h_k, s_k = grouped[g]
@@ -164,22 +167,21 @@ def tile_stackrnn_pa_t_kernel(
             )
             quantised[g] = (x_codes, x_scales, h_codes, h_scales)
 
-        def stack_product_group(g):
+        def stack_product_tile(g, r, transpose_ahead):
             s_k = grouped[g][2]
-            pre = results.tile([P, GROUP_TILES, HDIM], F32, name="pre")
-            for r in range(GROUP_TILES):
-                stack_ps = psum_two.tile([P, HDIM], F32, name="stack_ps")
-                for e in range(2):
-                    nc.tensor.matmul(
-                        out=stack_ps[:], lhsT=s_k[:, r, :, e], rhs=w_stack[:, e, :], start=(e == 0), stop=(e == 1)
-                    )
-                nc.vector.tensor_tensor(out=pre[:, r, :], in0=stack_ps[:], in1=bias_all[:], op=ADD)
-            sums[g] = [pre]
+            stack_ps = psum.tile([P, HDIM], F32, name="stack_ps")
+            nc.tensor.matmul(out=stack_ps[:], lhsT=s_k[:, r, :, 0], rhs=w_stack[:, 0, :], start=True, stop=False)
+            if transpose_ahead:
+                x_t = transpose_x(g + 1, r)
+            nc.tensor.matmul(out=stack_ps[:], lhsT=s_k[:, r, :, 1], rhs=w_stack[:, 1, :], start=False, stop=True)
+            if transpose_ahead:
+                transposed[(g + 1, r)] = (x_t, transpose_hidden_and_stack(g + 1, r))
+            nc.vector.tensor_tensor(out=pre_act[g][:, r, :], in0=stack_ps[:], in1=bias_all[:], op=ADD)
 
         def mx_product_group(g):
             x_codes, x_scales, h_codes, h_scales = quantised[g]
             for r in range(GROUP_TILES):
-                mx_ps = psum_two.tile([P, HDIM], F32, name="mx_ps")
+                mx_ps = psum.tile([P, HDIM], F32, name="mx_ps")
                 for a in range(W_PASSES):
                     if a < X_PASSES:
                         codes, scales = x_codes[:, r, a, :], x_scales[:, r, a, :]
@@ -194,18 +196,20 @@ def tile_stackrnn_pa_t_kernel(
                         start=(a == 0),
                         stop=(a == W_PASSES - 1),
                     )
-                sums[g].append(mx_ps)
+                mx_sums[(g, r)] = mx_ps
 
-        def finish_group(g):
-            pre = sums[g][0]
+        def join_sums_group(g):
             for r in range(GROUP_TILES):
-                nc.vector.tensor_tensor(out=pre[:, r, :], in0=sums[g][1 + r][:], in1=pre[:, r, :], op=ADD)
-                nc.scalar.activation(out=pre[:, r, :], in_=pre[:, r, :], func=SIGMOID)
-            nc.scalar.dma_start(out=out_tiles[:, g * GROUP_TILES : (g + 1) * GROUP_TILES, :], in_=pre[:])
+                nc.vector.tensor_tensor(
+                    out=pre_act[g][:, r, :], in0=mx_sums[(g, r)][:], in1=pre_act[g][:, r, :], op=ADD
+                )
 
-        copy_out_group(0, *transpose_group(0))
+        new_grouped_tiles(0)
+        for r in range(GROUP_TILES):
+            transposed[(0, r)] = (transpose_x(0, r), transpose_hidden_and_stack(0, r))
+            copy_out_tile(0, r)
 
-        w_cat_t = psum_two.tile([P, OUT_BLOCKS, P], F32, tag="stack_ps")
+        w_cat_t = psum.tile([P, OUT_BLOCKS, P], F32, tag="stack_ps")
         for j in range(OUT_BLOCKS):
             nc.tensor.transpose(w_cat_t[:, j, :], w_cat[:, j, :].bitcast(F32), identity[:])
         w_stack = consts.tile([P, 2, HDIM], BF16)
@@ -213,17 +217,28 @@ def tile_stackrnn_pa_t_kernel(
             out=w_stack[:],
             in_=w_cat_t[:].rearrange("p j n -> p (j n)").bitcast(BF16).rearrange("p (n e) -> p e n", e=2),
         )
-        bias_ps = psum_two.tile([P, HDIM], F32, tag="stack_ps")
+        bias_ps = psum.tile([P, HDIM], F32, tag="stack_ps")
         nc.tensor.matmul(out=bias_ps[:], lhsT=ones[:], rhs=bias_rows[:], start=True, stop=True)
         bias_all = consts.tile([P, HDIM], F32)
         nc.vector.tensor_copy(out=bias_all[:], in_=bias_ps[:])
 
-        for g in range(GROUPS):
+        for g in range(GROUPS + 2):
+            if g < GROUPS:
+                quantise_group(g)
+                pre_act[g] = results.tile([P, GROUP_TILES, HDIM], F32, name="pre")
+            if 1 <= g <= GROUPS:
+                join_sums_group(g - 1)
             if g + 1 < GROUPS:
-                copy_out_group(g + 1, *transpose_group(g + 1))
-            quantise_group(g)
-            if g > 0:
-                finish_group(g - 1)
-            stack_product_group(g)
-            mx_product_group(g)
-        finish_group(GROUPS - 1)
+                new_grouped_tiles(g + 1)
+            for r in range(GROUP_TILES):
+                if g >= 2:
+                    nc.scalar.activation(out=pre_act[g - 2][:, r, :], in_=pre_act[g - 2][:, r, :], func=SIGMOID)
+                if g < GROUPS:
+                    stack_product_tile(g, r, transpose_ahead=(g + 1 < GROUPS))
+                if g + 1 < GROUPS:
+                    copy_out_tile(g + 1, r)
+            if g >= 2:
+                tiles_of_group = slice((g - 2) * GROUP_TILES, (g - 1) * GROUP_TILES)
+                nc.scalar.dma_start(out=out_tiles[:, tiles_of_group, :], in_=pre_act[g - 2][:])
+            if g < GROUPS:
+                mx_product_group(g)

@@ -44,6 +44,7 @@ def tile_stackrnn_pa_t_kernel(
         consts = ctx.enter_context(tc.tile_pool(name="consts", bufs=1))
         inputs = ctx.enter_context(tc.tile_pool(name="inputs", bufs=GROUPS))
         work = ctx.enter_context(tc.tile_pool(name="work", bufs=2))
+        sorted_pool = ctx.enter_context(tc.tile_pool(name="sorted", bufs=3))
         results = ctx.enter_context(tc.tile_pool(name="results", bufs=5))
         psum = ctx.enter_context(tc.psum_pool(name="psum", bufs=GROUP_TILES))
 
@@ -105,6 +106,7 @@ def tile_stackrnn_pa_t_kernel(
             nc.scalar.dma_start(out=bias_rows[row : row + 1, :], in_=bias.rearrange("(o n) -> o n", o=1))
         nc.scalar.activation(out=zero_column[:], in_=zero_column[:], func=SIGMOID)
 
+        x_sorted = {}
         transposed = {}
         grouped = {}
         quantised = {}
@@ -112,13 +114,21 @@ def tile_stackrnn_pa_t_kernel(
         mx_sums = {}
         words_in_pass = K_PASS // 2
 
-        def transpose_x(g, r):
+        def new_sorted_tile(g):
+            x_sorted[g] = sorted_pool.tile([P, GROUP_TILES, X_PASSES, HALVES, P], F32, name="x_sorted")
+
+        def sort_x_tile(g, r):
             x_words = x_in[g][:].bitcast(F32)
+            nc.vector.tensor_copy(
+                out=x_sorted[g][:, r],
+                in_=x_words[:, r, :].rearrange("p (a c u) -> p a u c", a=X_PASSES, u=HALVES),
+            )
+
+        def transpose_x(g, r):
             x_t = psum.tile([P, X_PASSES, HALVES, P], F32, name="x_t")
             for a in range(X_PASSES):
                 for u in range(HALVES):
-                    every_second = slice(a * words_in_pass + u, (a + 1) * words_in_pass, HALVES)
-                    nc.tensor.transpose(x_t[:, a, u, :], x_words[:, r, every_second], identity[:])
+                    nc.tensor.transpose(x_t[:, a, u, :], x_sorted[g][:, r, a, u, :], identity[:])
             return x_t
 
         def transpose_hidden_and_stack(g, r):
@@ -205,6 +215,10 @@ def tile_stackrnn_pa_t_kernel(
                 )
 
         new_grouped_tiles(0)
+        new_sorted_tile(0)
+        new_sorted_tile(1)
+        for r in range(GROUP_TILES):
+            sort_x_tile(0, r)
         for r in range(GROUP_TILES):
             transposed[(0, r)] = (transpose_x(0, r), transpose_hidden_and_stack(0, r))
             copy_out_tile(0, r)
@@ -221,6 +235,8 @@ def tile_stackrnn_pa_t_kernel(
         nc.tensor.matmul(out=bias_ps[:], lhsT=ones[:], rhs=bias_rows[:], start=True, stop=True)
         bias_all = consts.tile([P, HDIM], F32)
         nc.vector.tensor_copy(out=bias_all[:], in_=bias_ps[:])
+        for r in range(GROUP_TILES):
+            sort_x_tile(1, r)
 
         for g in range(GROUPS + 2):
             if g < GROUPS:
@@ -230,7 +246,11 @@ def tile_stackrnn_pa_t_kernel(
                 join_sums_group(g - 1)
             if g + 1 < GROUPS:
                 new_grouped_tiles(g + 1)
+            if g + 2 < GROUPS:
+                new_sorted_tile(g + 2)
             for r in range(GROUP_TILES):
+                if g + 2 < GROUPS:
+                    sort_x_tile(g + 2, r)
                 if g >= 2:
                     nc.scalar.activation(out=pre_act[g - 2][:, r, :], in_=pre_act[g - 2][:, r, :], func=SIGMOID)
                 if g < GROUPS:

@@ -26,6 +26,7 @@ TILES = BATCH // P
 GROUP_TILES = 2
 GROUPS = TILES // GROUP_TILES
 OUT_BLOCKS = HDIM // P
+LOAD_AHEAD = 6
 
 FLOPS = 2 * BATCH * HDIM * (IDIM + HDIM + STACK)
 
@@ -44,9 +45,10 @@ def tile_stackrnn_pa_t_kernel(
         consts = ctx.enter_context(tc.tile_pool(name="consts", bufs=1))
         inputs = ctx.enter_context(tc.tile_pool(name="inputs", bufs=GROUPS))
         work = ctx.enter_context(tc.tile_pool(name="work", bufs=2))
-        sorted_pool = ctx.enter_context(tc.tile_pool(name="sorted", bufs=3))
+        sorted_pool = ctx.enter_context(tc.tile_pool(name="sorted", bufs=3 * GROUP_TILES))
         results = ctx.enter_context(tc.tile_pool(name="results", bufs=5))
         psum = ctx.enter_context(tc.psum_pool(name="psum", bufs=GROUP_TILES))
+        psum_group = ctx.enter_context(tc.psum_pool(name="psum_group", bufs=1))
 
         w_scales = consts.tile([P, W_PASSES, HDIM], U8, align_bytes=64)
         nc.vector.memset(w_scales[:].rearrange("p a n -> p (a n)").bitcast(I32), 0)
@@ -96,7 +98,7 @@ def tile_stackrnn_pa_t_kernel(
                 in_=Wh_scales[:, rows, :].bitcast(I32).rearrange("g r n -> r g n"),
             )
 
-        for g in range(1, GROUPS):
+        for g in range(1, LOAD_AHEAD):
             load_group(g)
 
         w_cat = consts.tile([P, OUT_BLOCKS, STACK], BF16)
@@ -107,57 +109,67 @@ def tile_stackrnn_pa_t_kernel(
         nc.scalar.activation(out=zero_column[:], in_=zero_column[:], func=SIGMOID)
 
         x_sorted = {}
-        transposed = {}
+        x_turned = {}
+        h_turned = {}
+        s_turned = {}
         grouped = {}
         quantised = {}
         pre_act = {}
         mx_sums = {}
         words_in_pass = K_PASS // 2
 
-        def new_sorted_tile(g):
-            x_sorted[g] = sorted_pool.tile([P, GROUP_TILES, X_PASSES, HALVES, P], F32, name="x_sorted")
-
-        def sort_x_tile(g, r):
-            x_words = x_in[g][:].bitcast(F32)
-            nc.vector.tensor_copy(
-                out=x_sorted[g][:, r],
-                in_=x_words[:, r, :].rearrange("p (a c u) -> p a u c", a=X_PASSES, u=HALVES),
-            )
+        def sort_x_group(g):
+            for r, copy in enumerate((nc.vector.tensor_copy, nc.scalar.copy)):
+                x_s = sorted_pool.tile([P, X_PASSES, HALVES, P], F32, name="x_sorted")
+                copy(
+                    out=x_s[:],
+                    in_=x_in[g][:, r, :].bitcast(F32).rearrange("p (a c u) -> p a u c", a=X_PASSES, u=HALVES),
+                )
+                x_sorted[(g, r)] = x_s
 
         def transpose_x(g, r):
             x_t = psum.tile([P, X_PASSES, HALVES, P], F32, name="x_t")
             for a in range(X_PASSES):
                 for u in range(HALVES):
-                    nc.tensor.transpose(x_t[:, a, u, :], x_sorted[g][:, r, a, u, :], identity[:])
-            return x_t
+                    nc.tensor.transpose(x_t[:, a, u, :], x_sorted[(g, r)][:, a, u, :], identity[:])
+            x_turned[(g, r)] = x_t
 
-        def transpose_hidden_and_stack(g, r):
-            h_words = h_in[g][:].bitcast(F32)
+        def transpose_stack(g):
             s_words = s_in[g][:].bitcast(F32)
-            hs_t = psum.tile([P, HALVES + 1, P], F32, name="hs_t")
-            for u in range(HALVES):
-                nc.tensor.transpose(hs_t[:, u, :], h_words[:, r, u:words_in_pass:HALVES], identity[:])
-            nc.tensor.transpose(hs_t[:, HALVES, :], s_words[:, r, :], identity[:])
-            return hs_t
+            for r in range(GROUP_TILES):
+                nc.tensor.transpose(s_turned[g][:, r, :], s_words[:, r, :], identity[:])
 
-        def new_grouped_tiles(g):
+        def transpose_hidden(g):
+            h_words = h_in[g][:].bitcast(F32)
+            for r in range(GROUP_TILES):
+                for u in range(HALVES):
+                    nc.tensor.transpose(h_turned[g][:, r, u, :], h_words[:, r, u:words_in_pass:HALVES], identity[:])
+
+        def new_group_tiles(g):
+            h_turned[g] = psum_group.tile([P, GROUP_TILES, HALVES, P], F32, name="h_t")
+            s_turned[g] = psum_group.tile([P, GROUP_TILES, HALVES, P], F32, name="s_t")[:, :, 0, :]
             x_k = work.tile([P, GROUP_TILES, X_PASSES, P, PACK], BF16, name="x_k", align_bytes=64)
             h_k = work.tile([P, GROUP_TILES, P, PACK], BF16, name="h_k", align_bytes=64)
             s_k = work.tile([P, GROUP_TILES, P, 2], BF16, name="s_k")
             grouped[g] = (x_k, h_k, s_k)
 
-        def copy_out_tile(g, r):
-            x_k, h_k, s_k = grouped[g]
-            x_t, hs_t = transposed[(g, r)]
+        def copy_out_x(g, r):
+            x_k = grouped[g][0]
             nc.scalar.copy(
                 out=x_k[:, r].rearrange("p a c t -> p a (c t)").bitcast(F32).rearrange("p a (c u) -> p a c u", u=HALVES),
-                in_=x_t[:].rearrange("p a u c -> p a c u"),
+                in_=x_turned[(g, r)][:].rearrange("p a u c -> p a c u"),
             )
+
+        def copy_out_hidden(g):
+            h_k = grouped[g][1]
             nc.scalar.copy(
-                out=h_k[:, r].rearrange("p c t -> p (c t)").bitcast(F32).rearrange("p (c u) -> p c u", u=HALVES),
-                in_=hs_t[:, 0:HALVES, :].rearrange("p u c -> p c u"),
+                out=h_k[:].rearrange("p r c t -> p r (c t)").bitcast(F32).rearrange("p r (c u) -> p r c u", u=HALVES),
+                in_=h_turned[g][:].rearrange("p r u c -> p r c u"),
             )
-            nc.scalar.copy(out=s_k[:, r].rearrange("p c e -> p (c e)").bitcast(F32), in_=hs_t[:, HALVES, :])
+
+        def copy_out_stack(g):
+            s_k = grouped[g][2]
+            nc.scalar.copy(out=s_k[:].rearrange("p r c e -> p r (c e)").bitcast(F32), in_=s_turned[g])
 
         def quantise_group(g):
             x_k, h_k, s_k = grouped[g]
@@ -182,10 +194,12 @@ def tile_stackrnn_pa_t_kernel(
             stack_ps = psum.tile([P, HDIM], F32, name="stack_ps")
             nc.tensor.matmul(out=stack_ps[:], lhsT=s_k[:, r, :, 0], rhs=w_stack[:, 0, :], start=True, stop=False)
             if transpose_ahead:
-                x_t = transpose_x(g + 1, r)
+                transpose_x(g + 1, r)
             nc.tensor.matmul(out=stack_ps[:], lhsT=s_k[:, r, :, 1], rhs=w_stack[:, 1, :], start=False, stop=True)
-            if transpose_ahead:
-                transposed[(g + 1, r)] = (x_t, transpose_hidden_and_stack(g + 1, r))
+            if transpose_ahead and r == 0:
+                transpose_stack(g + 1)
+            if transpose_ahead and r == 1:
+                transpose_hidden(g + 1)
             nc.vector.tensor_tensor(out=pre_act[g][:, r, :], in0=stack_ps[:], in1=bias_all[:], op=ADD)
 
         def mx_product_group(g):
@@ -214,14 +228,23 @@ def tile_stackrnn_pa_t_kernel(
                     out=pre_act[g][:, r, :], in0=mx_sums[(g, r)][:], in1=pre_act[g][:, r, :], op=ADD
                 )
 
-        new_grouped_tiles(0)
-        new_sorted_tile(0)
-        new_sorted_tile(1)
+        def sigmoid_group(g):
+            sums = pre_act[g][:].rearrange("p r n -> p (r n)")
+            nc.scalar.activation(out=sums, in_=sums, func=SIGMOID)
+
+        def store_group(g):
+            tiles_of_g = slice(g * GROUP_TILES, (g + 1) * GROUP_TILES)
+            nc.sync.dma_start(out=out_tiles[:, tiles_of_g, :], in_=pre_act[g][:])
+
+        sort_x_group(0)
+        new_group_tiles(0)
         for r in range(GROUP_TILES):
-            sort_x_tile(0, r)
-        for r in range(GROUP_TILES):
-            transposed[(0, r)] = (transpose_x(0, r), transpose_hidden_and_stack(0, r))
-            copy_out_tile(0, r)
+            transpose_x(0, r)
+            copy_out_x(0, r)
+        transpose_stack(0)
+        copy_out_stack(0)
+        transpose_hidden(0)
+        copy_out_hidden(0)
 
         w_cat_t = psum.tile([P, OUT_BLOCKS, P], F32, tag="stack_ps")
         for j in range(OUT_BLOCKS):
@@ -235,30 +258,32 @@ def tile_stackrnn_pa_t_kernel(
         nc.tensor.matmul(out=bias_ps[:], lhsT=ones[:], rhs=bias_rows[:], start=True, stop=True)
         bias_all = consts.tile([P, HDIM], F32)
         nc.vector.tensor_copy(out=bias_all[:], in_=bias_ps[:])
-        for r in range(GROUP_TILES):
-            sort_x_tile(1, r)
+        sort_x_group(1)
 
         for g in range(GROUPS + 2):
+            if g + LOAD_AHEAD < GROUPS:
+                load_group(g + LOAD_AHEAD)
             if g < GROUPS:
                 quantise_group(g)
                 pre_act[g] = results.tile([P, GROUP_TILES, HDIM], F32, name="pre")
             if 1 <= g <= GROUPS:
                 join_sums_group(g - 1)
-            if g + 1 < GROUPS:
-                new_grouped_tiles(g + 1)
             if g + 2 < GROUPS:
-                new_sorted_tile(g + 2)
+                sort_x_group(g + 2)
+            if g + 1 < GROUPS:
+                new_group_tiles(g + 1)
             for r in range(GROUP_TILES):
-                if g + 2 < GROUPS:
-                    sort_x_tile(g + 2, r)
-                if g >= 2:
-                    nc.scalar.activation(out=pre_act[g - 2][:, r, :], in_=pre_act[g - 2][:, r, :], func=SIGMOID)
                 if g < GROUPS:
                     stack_product_tile(g, r, transpose_ahead=(g + 1 < GROUPS))
                 if g + 1 < GROUPS:
-                    copy_out_tile(g + 1, r)
+                    copy_out_x(g + 1, r)
+                if r == 0 and g + 1 < GROUPS:
+                    copy_out_stack(g + 1)
+                if r == 0 and g >= 2:
+                    sigmoid_group(g - 2)
+            if g + 1 < GROUPS:
+                copy_out_hidden(g + 1)
             if g >= 2:
-                tiles_of_group = slice((g - 2) * GROUP_TILES, (g - 1) * GROUP_TILES)
-                nc.scalar.dma_start(out=out_tiles[:, tiles_of_group, :], in_=pre_act[g - 2][:])
+                store_group(g - 2)
             if g < GROUPS:
                 mx_product_group(g)

@@ -27,6 +27,7 @@ GROUP_TILES = 2
 GROUPS = TILES // GROUP_TILES
 OUT_BLOCKS = HDIM // P
 LOAD_AHEAD = 6
+LAST_PIECE = HDIM // 2
 
 FLOPS = 2 * BATCH * HDIM * (IDIM + HDIM + STACK)
 
@@ -139,11 +140,9 @@ def tile_stackrnn_pa_t_kernel(
             for r in range(GROUP_TILES):
                 nc.tensor.transpose(s_turned[g][:, r, :], s_words[:, r, :], identity[:])
 
-        def transpose_hidden(g):
+        def transpose_hidden(g, r, u):
             h_words = h_in[g][:].bitcast(F32)
-            for r in range(GROUP_TILES):
-                for u in range(HALVES):
-                    nc.tensor.transpose(h_turned[g][:, r, u, :], h_words[:, r, u:words_in_pass:HALVES], identity[:])
+            nc.tensor.transpose(h_turned[g][:, r, u, :], h_words[:, r, u:words_in_pass:HALVES], identity[:])
 
         def new_group_tiles(g):
             h_turned[g] = psum_group.tile([P, GROUP_TILES, HALVES, P], F32, name="h_t")
@@ -194,12 +193,13 @@ def tile_stackrnn_pa_t_kernel(
             stack_ps = psum.tile([P, HDIM], F32, name="stack_ps")
             nc.tensor.matmul(out=stack_ps[:], lhsT=s_k[:, r, :, 0], rhs=w_stack[:, 0, :], start=True, stop=False)
             if transpose_ahead:
+                transpose_hidden(g + 1, r, 0)
                 transpose_x(g + 1, r)
             nc.tensor.matmul(out=stack_ps[:], lhsT=s_k[:, r, :, 1], rhs=w_stack[:, 1, :], start=False, stop=True)
+            if transpose_ahead:
+                transpose_hidden(g + 1, r, 1)
             if transpose_ahead and r == 0:
                 transpose_stack(g + 1)
-            if transpose_ahead and r == 1:
-                transpose_hidden(g + 1)
             nc.vector.tensor_tensor(out=pre_act[g][:, r, :], in0=stack_ps[:], in1=bias_all[:], op=ADD)
 
         def mx_product_group(g):
@@ -236,6 +236,15 @@ def tile_stackrnn_pa_t_kernel(
             tiles_of_g = slice(g * GROUP_TILES, (g + 1) * GROUP_TILES)
             nc.sync.dma_start(out=out_tiles[:, tiles_of_g, :], in_=pre_act[g][:])
 
+        def finish_in_pieces(g):
+            for r in range(GROUP_TILES):
+                for first in range(0, HDIM, LAST_PIECE):
+                    cols = slice(first, first + LAST_PIECE)
+                    piece = pre_act[g][:, r, cols]
+                    nc.vector.tensor_tensor(out=piece, in0=mx_sums[(g, r)][:, cols], in1=piece, op=ADD)
+                    nc.scalar.activation(out=piece, in_=piece, func=SIGMOID)
+                    nc.sync.dma_start(out=out_tiles[:, g * GROUP_TILES + r, cols], in_=piece)
+
         sort_x_group(0)
         new_group_tiles(0)
         for r in range(GROUP_TILES):
@@ -243,7 +252,9 @@ def tile_stackrnn_pa_t_kernel(
             copy_out_x(0, r)
         transpose_stack(0)
         copy_out_stack(0)
-        transpose_hidden(0)
+        for r in range(GROUP_TILES):
+            for u in range(HALVES):
+                transpose_hidden(0, r, u)
         copy_out_hidden(0)
 
         w_cat_t = psum.tile([P, OUT_BLOCKS, P], F32, tag="stack_ps")
@@ -260,13 +271,13 @@ def tile_stackrnn_pa_t_kernel(
         nc.vector.tensor_copy(out=bias_all[:], in_=bias_ps[:])
         sort_x_group(1)
 
-        for g in range(GROUPS + 2):
+        for g in range(GROUPS + 1):
             if g + LOAD_AHEAD < GROUPS:
                 load_group(g + LOAD_AHEAD)
             if g < GROUPS:
                 quantise_group(g)
                 pre_act[g] = results.tile([P, GROUP_TILES, HDIM], F32, name="pre")
-            if 1 <= g <= GROUPS:
+            if 1 <= g < GROUPS:
                 join_sums_group(g - 1)
             if g + 2 < GROUPS:
                 sort_x_group(g + 2)
@@ -287,3 +298,4 @@ def tile_stackrnn_pa_t_kernel(
                 store_group(g - 2)
             if g < GROUPS:
                 mx_product_group(g)
+        finish_in_pieces(GROUPS - 1)

@@ -290,10 +290,10 @@ def tile_stackrnn_pa_t_kernel(
                     copy_out_x(g + 1, r)
                 if r == 0 and g + 1 < GROUPS:
                     copy_out_stack(g + 1)
-                if r == 0 and g >= 2:
-                    sigmoid_group(g - 2)
             if g + 1 < GROUPS:
                 copy_out_hidden(g + 1)
+            if g >= 2:
+                sigmoid_group(g - 2)
             if g >= 2:
                 store_group(g - 2)
             if g < GROUPS:

@@ -11,6 +11,7 @@ U8 = mybir.dt.uint8
 FP8X4 = mybir.dt.float8_e4m3fn_x4
 FP4X4 = mybir.dt.float4_e2m1fn_x4
 ADD = mybir.AluOpType.add
+MULT = mybir.AluOpType.mult
 SIGMOID = mybir.ActivationFunctionType.Sigmoid
 
 P = 128
@@ -59,6 +60,7 @@ def tile_stackrnn_pa_t_kernel(
         nc.vector.memset(ones[:], 1.0)
         zero_column = consts.tile([P, 1], F32)
         nc.vector.memset(zero_column[:], 0.0)
+        port_turn = consts.tile([P, 1], F32)
         identity = consts.tile([P, P], F32)
         make_identity(nc, identity[:])
 
@@ -77,6 +79,7 @@ def tile_stackrnn_pa_t_kernel(
             s_in.append(s_g)
 
         load_group(0)
+        load_group(1)
 
         w_words = consts.tile([P, W_PASSES, 2 * HDIM], U8, align_bytes=64)
         nc.sync.dma_start(
@@ -99,7 +102,7 @@ def tile_stackrnn_pa_t_kernel(
                 in_=Wh_scales[:, rows, :].bitcast(I32).rearrange("g r n -> r g n"),
             )
 
-        for g in range(1, LOAD_AHEAD):
+        for g in range(2, LOAD_AHEAD):
             load_group(g)
 
         w_cat = consts.tile([P, OUT_BLOCKS, STACK], BF16)
@@ -119,14 +122,30 @@ def tile_stackrnn_pa_t_kernel(
         mx_sums = {}
         words_in_pass = K_PASS // 2
 
-        def sort_x_group(g):
-            for r, copy in enumerate((nc.vector.tensor_copy, nc.scalar.copy)):
+        def sort_x_group(g, pipeline_runs):
+            for r in range(GROUP_TILES):
                 x_s = sorted_pool.tile([P, X_PASSES, HALVES, P], F32, name="x_sorted")
-                copy(
-                    out=x_s[:],
-                    in_=x_in[g][:, r, :].bitcast(F32).rearrange("p (a c u) -> p a u c", a=X_PASSES, u=HALVES),
-                )
                 x_sorted[(g, r)] = x_s
+                words = x_in[g][:, r, :].bitcast(F32).rearrange("p (a c u) -> p a u c", a=X_PASSES, u=HALVES)
+                if r == 0:
+                    nc.vector.tensor_copy(out=x_s[:], in_=words)
+                elif not pipeline_runs:
+                    nc.scalar.copy(out=x_s[:], in_=words)
+                else:
+                    nc.gpsimd.tensor_copy(out=port_turn[:], in_=x_sorted[(g, 0)][:, 0, 0, 0:1])
+                    for a in range(X_PASSES):
+                        nc.gpsimd.tensor_scalar(
+                            out=x_s[:, a].rearrange("p u c -> p (u c)").bitcast(BF16).rearrange(
+                                "p (u c e) -> p u c e", u=HALVES, e=2
+                            ),
+                            in0=x_in[g][:, r, a * K_PASS : (a + 1) * K_PASS].rearrange(
+                                "p (c u e) -> p u c e", u=HALVES, e=2
+                            ),
+                            scalar1=1.0,
+                            scalar2=0.0,
+                            op0=MULT,
+                            op1=ADD,
+                        )
 
         def transpose_x(g, r):
             x_t = psum.tile([P, X_PASSES, HALVES, P], F32, name="x_t")
@@ -245,7 +264,7 @@ def tile_stackrnn_pa_t_kernel(
                     nc.scalar.activation(out=piece, in_=piece, func=SIGMOID)
                     nc.sync.dma_start(out=out_tiles[:, g * GROUP_TILES + r, cols], in_=piece)
 
-        sort_x_group(0)
+        sort_x_group(0, pipeline_runs=False)
         new_group_tiles(0)
         for r in range(GROUP_TILES):
             transpose_x(0, r)
@@ -269,7 +288,7 @@ def tile_stackrnn_pa_t_kernel(
         nc.tensor.matmul(out=bias_ps[:], lhsT=ones[:], rhs=bias_rows[:], start=True, stop=True)
         bias_all = consts.tile([P, HDIM], F32)
         nc.vector.tensor_copy(out=bias_all[:], in_=bias_ps[:])
-        sort_x_group(1)
+        sort_x_group(1, pipeline_runs=False)
 
         for g in range(GROUPS + 1):
             if g + LOAD_AHEAD < GROUPS:
@@ -277,10 +296,10 @@ def tile_stackrnn_pa_t_kernel(
             if g < GROUPS:
                 quantise_group(g)
                 pre_act[g] = results.tile([P, GROUP_TILES, HDIM], F32, name="pre")
+            if g + 2 < GROUPS:
+                sort_x_group(g + 2, pipeline_runs=True)
             if 1 <= g < GROUPS:
                 join_sums_group(g - 1)
-            if g + 2 < GROUPS:
-                sort_x_group(g + 2)
             if g + 1 < GROUPS:
                 new_group_tiles(g + 1)
             for r in range(GROUP_TILES):

@@ -28,6 +28,7 @@ GROUP_TILES = 2
 GROUPS = TILES // GROUP_TILES
 OUT_BLOCKS = HDIM // P
 LOAD_AHEAD = 6
+WARM_UP_MATMULS = 6
 LAST_PIECE = HDIM // 2
 
 FLOPS = 2 * BATCH * HDIM * (IDIM + HDIM + STACK)
@@ -63,6 +64,11 @@ def tile_stackrnn_pa_t_kernel(
         port_turn = consts.tile([P, 1], F32)
         identity = consts.tile([P, P], F32)
         make_identity(nc, identity[:])
+        zeros = consts.tile([P, HDIM], BF16)
+        nc.vector.memset(zeros[:], 0.0)
+        warm_ps = psum.tile([P, HDIM], F32, tag="mx_ps")
+        for i in range(WARM_UP_MATMULS):
+            nc.tensor.matmul(out=warm_ps[:], lhsT=ones[:], rhs=zeros[:], start=True, stop=True)
 
         x_in, h_in, s_in = [], [], []
 
@@ -80,6 +86,8 @@ def tile_stackrnn_pa_t_kernel(
 
         load_group(0)
         load_group(1)
+        for row, bias in enumerate((bi, bh, b0, b1)):
+            nc.sync.dma_start(out=bias_rows[row : row + 1, :], in_=bias.rearrange("(o n) -> o n", o=1))
 
         w_words = consts.tile([P, W_PASSES, 2 * HDIM], U8, align_bytes=64)
         nc.sync.dma_start(
@@ -108,8 +116,6 @@ def tile_stackrnn_pa_t_kernel(
         w_cat = consts.tile([P, OUT_BLOCKS, STACK], BF16)
         nc.scalar.dma_start(out=w_cat[:, :, 0 : STACK // 2], in_=W0.rearrange("(j n) s -> n j s", n=P))
         nc.scalar.dma_start(out=w_cat[:, :, STACK // 2 : STACK], in_=W1.rearrange("(j n) s -> n j s", n=P))
-        for row, bias in enumerate((bi, bh, b0, b1)):
-            nc.scalar.dma_start(out=bias_rows[row : row + 1, :], in_=bias.rearrange("(o n) -> o n", o=1))
         nc.scalar.activation(out=zero_column[:], in_=zero_column[:], func=SIGMOID)
 
         x_sorted = {}

@@ -134,7 +134,8 @@ def tile_stackrnn_pa_t_kernel(
                 x_sorted[(g, r)] = x_s
                 words = x_in[g][:, r, :].bitcast(F32).rearrange("p (a c u) -> p a u c", a=X_PASSES, u=HALVES)
                 if r == 0:
-                    nc.vector.tensor_copy(out=x_s[:], in_=words)
+                    nc.vector.tensor_copy(out=x_s[:, 0], in_=words[:, 0])
+                    nc.scalar.copy(out=x_s[:, 1], in_=words[:, 1])
                 elif not pipeline_runs:
                     nc.scalar.copy(out=x_s[:], in_=words)
                 else:

@@ -28,7 +28,7 @@ GROUP_TILES = 2
 GROUPS = TILES // GROUP_TILES
 OUT_BLOCKS = HDIM // P
 LOAD_AHEAD = 6
-WARM_UP_MATMULS = 6
+WARM_UP_MATMULS = 4
 LAST_PIECE = HDIM // 2
 
 FLOPS = 2 * BATCH * HDIM * (IDIM + HDIM + STACK)
@@ -53,43 +53,64 @@ def tile_stackrnn_pa_t_kernel(
         psum = ctx.enter_context(tc.psum_pool(name="psum", bufs=GROUP_TILES))
         psum_group = ctx.enter_context(tc.psum_pool(name="psum_group", bufs=1))
 
-        w_scales = consts.tile([P, W_PASSES, HDIM], U8, align_bytes=64)
-        nc.vector.memset(w_scales[:].rearrange("p a n -> p (a n)").bitcast(I32), 0)
-        bias_rows = consts.tile([P, HDIM], BF16)
-        nc.vector.memset(bias_rows[:], 0.0)
         ones = consts.tile([P, P], BF16)
         nc.vector.memset(ones[:], 1.0)
+        zeros = consts.tile([P, HDIM], BF16)
+        nc.vector.memset(zeros[:], 0.0)
+        bias_rows = consts.tile([P, HDIM], BF16)
+        nc.vector.memset(bias_rows[:], 0.0)
+        w_scales = consts.tile([P, W_PASSES, HDIM], U8, align_bytes=64)
+        nc.vector.memset(w_scales[:].rearrange("p a n -> p (a n)").bitcast(I32), 0)
         zero_column = consts.tile([P, 1], F32)
         nc.vector.memset(zero_column[:], 0.0)
         port_turn = consts.tile([P, 1], F32)
         identity = consts.tile([P, P], F32)
         make_identity(nc, identity[:])
-        zeros = consts.tile([P, HDIM], BF16)
-        nc.vector.memset(zeros[:], 0.0)
         warm_ps = psum.tile([P, HDIM], F32, tag="mx_ps")
         for i in range(WARM_UP_MATMULS):
             nc.tensor.matmul(out=warm_ps[:], lhsT=ones[:], rhs=zeros[:], start=True, stop=True)
 
         x_in, h_in, s_in = [], [], []
 
-        def load_group(g):
+        def load_group(g, behind_x=None):
             tiles_of_g = slice(g * GROUP_TILES, (g + 1) * GROUP_TILES)
             x_g = inputs.tile([P, GROUP_TILES, IDIM], BF16, name="x_g")
             nc.sync.dma_start(out=x_g[:], in_=x_tiles[:, tiles_of_g, :])
-            h_g = inputs.tile([P, GROUP_TILES, HDIM], BF16, name="h_g")
-            nc.sync.dma_start(out=h_g[:], in_=h_tiles[:, tiles_of_g, :])
+            if behind_x:
+                behind_x()
             s_g = inputs.tile([P, GROUP_TILES, STACK], BF16, name="s_g")
             nc.sync.dma_start(out=s_g[:], in_=s_tiles[:, tiles_of_g, :])
+            h_g = inputs.tile([P, GROUP_TILES, HDIM], BF16, name="h_g")
+            nc.sync.dma_start(out=h_g[:], in_=h_tiles[:, tiles_of_g, :])
             x_in.append(x_g)
             h_in.append(h_g)
             s_in.append(s_g)
 
-        load_group(0)
-        load_group(1)
         for row, bias in enumerate((bi, bh, b0, b1)):
-            nc.sync.dma_start(out=bias_rows[row : row + 1, :], in_=bias.rearrange("(o n) -> o n", o=1))
+            nc.gpsimd.dma_start(out=bias_rows[row : row + 1, :], in_=bias.rearrange("(o n) -> o n", o=1))
+        w_cat = consts.tile([P, OUT_BLOCKS, STACK], BF16)
+
+        def load_stack_weights():
+            nc.sync.dma_start(out=w_cat[:, :, 0 : STACK // 2], in_=W0.rearrange("(j n) s -> n j s", n=P))
+            nc.sync.dma_start(out=w_cat[:, :, STACK // 2 : STACK], in_=W1.rearrange("(j n) s -> n j s", n=P))
 
         w_words = consts.tile([P, W_PASSES, 2 * HDIM], U8, align_bytes=64)
+
+        def load_scales():
+            for quadrant in range(4):
+                rows = slice(4 * quadrant, 4 * quadrant + 4)
+                parts = slice(32 * quadrant, 32 * quadrant + 4)
+                nc.sync.dma_start(
+                    out=w_scales[parts, 0:X_PASSES, :].bitcast(I32),
+                    in_=Wi_scales[:, rows, :].bitcast(I32).rearrange("g r n -> r g n"),
+                )
+                nc.sync.dma_start(
+                    out=w_scales[parts, X_PASSES:W_PASSES, :].bitcast(I32),
+                    in_=Wh_scales[:, rows, :].bitcast(I32).rearrange("g r n -> r g n"),
+                )
+
+        load_group(0, behind_x=load_stack_weights)
+        load_group(1)
         nc.sync.dma_start(
             out=w_words[:, 0:X_PASSES, :].bitcast(I32),
             in_=Wi_words.bitcast(I32).rearrange("g p n -> p g n"),
@@ -98,24 +119,10 @@ def tile_stackrnn_pa_t_kernel(
             out=w_words[:, X_PASSES:W_PASSES, :].bitcast(I32),
             in_=Wh_words.bitcast(I32).rearrange("g p n -> p g n"),
         )
-        for quadrant in range(4):
-            rows = slice(4 * quadrant, 4 * quadrant + 4)
-            parts = slice(32 * quadrant, 32 * quadrant + 4)
-            nc.sync.dma_start(
-                out=w_scales[parts, 0:X_PASSES, :].bitcast(I32),
-                in_=Wi_scales[:, rows, :].bitcast(I32).rearrange("g r n -> r g n"),
-            )
-            nc.sync.dma_start(
-                out=w_scales[parts, X_PASSES:W_PASSES, :].bitcast(I32),
-                in_=Wh_scales[:, rows, :].bitcast(I32).rearrange("g r n -> r g n"),
-            )
-
-        for g in range(2, LOAD_AHEAD):
+        load_group(2, behind_x=load_scales)
+        for g in range(3, LOAD_AHEAD):
             load_group(g)
 
-        w_cat = consts.tile([P, OUT_BLOCKS, STACK], BF16)
-        nc.scalar.dma_start(out=w_cat[:, :, 0 : STACK // 2], in_=W0.rearrange("(j n) s -> n j s", n=P))
-        nc.scalar.dma_start(out=w_cat[:, :, STACK // 2 : STACK], in_=W1.rearrange("(j n) s -> n j s", n=P))
         nc.scalar.activation(out=zero_column[:], in_=zero_column[:], func=SIGMOID)
 
         x_sorted = {}
@@ -125,6 +132,7 @@ def tile_stackrnn_pa_t_kernel(
         grouped = {}
         quantised = {}
         pre_act = {}
+        stack_sums = {}
         mx_sums = {}
         words_in_pass = K_PASS // 2
 
@@ -135,7 +143,8 @@ def tile_stackrnn_pa_t_kernel(
                 words = x_in[g][:, r, :].bitcast(F32).rearrange("p (a c u) -> p a u c", a=X_PASSES, u=HALVES)
                 if r == 0:
                     nc.vector.tensor_copy(out=x_s[:, 0], in_=words[:, 0])
-                    nc.scalar.copy(out=x_s[:, 1], in_=words[:, 1])
+                    if not pipeline_runs:
+                        nc.scalar.copy(out=x_s[:, 1], in_=words[:, 1])
                 elif not pipeline_runs:
                     nc.scalar.copy(out=x_s[:], in_=words)
                 else:
@@ -154,11 +163,21 @@ def tile_stackrnn_pa_t_kernel(
                             op1=ADD,
                         )
 
+        def sort_x_on_scalar(g):
+            words = x_in[g][:, 0, :].bitcast(F32).rearrange("p (a c u) -> p a u c", a=X_PASSES, u=HALVES)
+            nc.scalar.copy(out=x_sorted[(g, 0)][:, 1], in_=words[:, 1])
+
         def transpose_x(g, r):
             x_t = psum.tile([P, X_PASSES, HALVES, P], F32, name="x_t")
             for a in range(X_PASSES):
                 for u in range(HALVES):
-                    nc.tensor.transpose(x_t[:, a, u, :], x_sorted[(g, r)][:, a, u, :], identity[:])
+                    if (g, r) in x_sorted:
+                        words = x_sorted[(g, r)][:, a, u, :]
+                    else:
+                        first = a * words_in_pass + u
+                        last = (a + 1) * words_in_pass
+                        words = x_in[g][:, r, :].bitcast(F32)[:, first:last:HALVES]
+                    nc.tensor.transpose(x_t[:, a, u, :], words, identity[:])
             x_turned[(g, r)] = x_t
 
         def transpose_stack(g):
@@ -185,9 +204,9 @@ def tile_stackrnn_pa_t_kernel(
                 in_=x_turned[(g, r)][:].rearrange("p a u c -> p a c u"),
             )
 
-        def copy_out_hidden(g):
+        def copy_out_hidden(g, copy=nc.scalar.copy):
             h_k = grouped[g][1]
-            nc.scalar.copy(
+            copy(
                 out=h_k[:].rearrange("p r c t -> p r (c t)").bitcast(F32).rearrange("p r (c u) -> p r c u", u=HALVES),
                 in_=h_turned[g][:].rearrange("p r u c -> p r c u"),
             )
@@ -226,27 +245,29 @@ def tile_stackrnn_pa_t_kernel(
                 transpose_hidden(g + 1, r, 1)
             if transpose_ahead and r == 0:
                 transpose_stack(g + 1)
-            nc.vector.tensor_tensor(out=pre_act[g][:, r, :], in0=stack_ps[:], in1=bias_all[:], op=ADD)
+            stack_sums[(g, r)] = stack_ps
 
-        def mx_product_group(g):
+        def add_biases(g, r):
+            nc.vector.tensor_tensor(out=pre_act[g][:, r, :], in0=stack_sums[(g, r)][:], in1=bias_all[:], op=ADD)
+
+        def mx_product_tile(g, r):
             x_codes, x_scales, h_codes, h_scales = quantised[g]
-            for r in range(GROUP_TILES):
-                mx_ps = psum.tile([P, HDIM], F32, name="mx_ps")
-                for a in range(W_PASSES):
-                    if a < X_PASSES:
-                        codes, scales = x_codes[:, r, a, :], x_scales[:, r, a, :]
-                    else:
-                        codes, scales = h_codes[:, r, :], h_scales[:, r, :]
-                    nc.tensor.matmul_mx(
-                        out=mx_ps[:],
-                        lhsT=codes.bitcast(FP8X4),
-                        lhsT_scale=scales,
-                        rhs=w_words[:, a, :].bitcast(FP4X4),
-                        rhs_scale=w_scales[:, a, :],
-                        start=(a == 0),
-                        stop=(a == W_PASSES - 1),
-                    )
-                mx_sums[(g, r)] = mx_ps
+            mx_ps = psum.tile([P, HDIM], F32, name="mx_ps")
+            for a in range(W_PASSES):
+                if a < X_PASSES:
+                    codes, scales = x_codes[:, r, a, :], x_scales[:, r, a, :]
+                else:
+                    codes, scales = h_codes[:, r, :], h_scales[:, r, :]
+                nc.tensor.matmul_mx(
+                    out=mx_ps[:],
+                    lhsT=codes.bitcast(FP8X4),
+                    lhsT_scale=scales,
+                    rhs=w_words[:, a, :].bitcast(FP4X4),
+                    rhs_scale=w_scales[:, a, :],
+                    start=(a == 0),
+                    stop=(a == W_PASSES - 1),
+                )
+            mx_sums[(g, r)] = mx_ps
 
         def join_sums_group(g):
             for r in range(GROUP_TILES):
@@ -271,30 +292,32 @@ def tile_stackrnn_pa_t_kernel(
                     nc.scalar.activation(out=piece, in_=piece, func=SIGMOID)
                     nc.sync.dma_start(out=out_tiles[:, g * GROUP_TILES + r, cols], in_=piece)
 
-        sort_x_group(0, pipeline_runs=False)
+        w_cat_t = psum.tile([P, OUT_BLOCKS, P], F32, tag="stack_ps")
+        w_stack = consts.tile([P, 2, HDIM], BF16)
         new_group_tiles(0)
-        for r in range(GROUP_TILES):
-            transpose_x(0, r)
-            copy_out_x(0, r)
+        transpose_x(0, 0)
+        copy_out_x(0, 0)
+        for j in range(OUT_BLOCKS):
+            nc.tensor.transpose(w_cat_t[:, j, :], w_cat[:, j, :].bitcast(F32), identity[:])
+        nc.vector.tensor_copy(
+            out=w_stack[:],
+            in_=w_cat_t[:].rearrange("p j n -> p (j n)").bitcast(BF16).rearrange("p (n e) -> p e n", e=2),
+        )
+        transpose_x(0, 1)
+        copy_out_x(0, 1)
         transpose_stack(0)
         copy_out_stack(0)
         for r in range(GROUP_TILES):
             for u in range(HALVES):
                 transpose_hidden(0, r, u)
-        copy_out_hidden(0)
-
-        w_cat_t = psum.tile([P, OUT_BLOCKS, P], F32, tag="stack_ps")
-        for j in range(OUT_BLOCKS):
-            nc.tensor.transpose(w_cat_t[:, j, :], w_cat[:, j, :].bitcast(F32), identity[:])
-        w_stack = consts.tile([P, 2, HDIM], BF16)
-        nc.vector.tensor_copy(
-            out=w_stack[:],
-            in_=w_cat_t[:].rearrange("p j n -> p (j n)").bitcast(BF16).rearrange("p (n e) -> p e n", e=2),
-        )
-        bias_ps = psum.tile([P, HDIM], F32, tag="stack_ps")
-        nc.tensor.matmul(out=bias_ps[:], lhsT=ones[:], rhs=bias_rows[:], start=True, stop=True)
+        copy_out_hidden(0, copy=nc.vector.tensor_copy)
         bias_all = consts.tile([P, HDIM], F32)
-        nc.vector.tensor_copy(out=bias_all[:], in_=bias_ps[:])
+
+        def add_up_biases():
+            bias_ps = psum_group.tile([P, HDIM], F32, tag="s_t")
+            nc.tensor.matmul(out=bias_ps[:], lhsT=ones[:], rhs=bias_rows[:], start=True, stop=True)
+            nc.vector.tensor_copy(out=bias_all[:], in_=bias_ps[:])
+
         sort_x_group(1, pipeline_runs=False)
 
         for g in range(GROUPS + 1):
@@ -303,8 +326,10 @@ def tile_stackrnn_pa_t_kernel(
             if g < GROUPS:
                 quantise_group(g)
                 pre_act[g] = results.tile([P, GROUP_TILES, HDIM], F32, name="pre")
-            if g + 2 < GROUPS:
+            if 1 <= g and g + 2 < GROUPS:
                 sort_x_group(g + 2, pipeline_runs=True)
+            if 2 <= g and g + 2 < GROUPS:
+                sort_x_on_scalar(g + 2)
             if 1 <= g < GROUPS:
                 join_sums_group(g - 1)
             if g + 1 < GROUPS:
@@ -312,16 +337,28 @@ def tile_stackrnn_pa_t_kernel(
             for r in range(GROUP_TILES):
                 if g < GROUPS:
                     stack_product_tile(g, r, transpose_ahead=(g + 1 < GROUPS))
+                if 0 < g < GROUPS:
+                    add_biases(g, r)
                 if g + 1 < GROUPS:
                     copy_out_x(g + 1, r)
                 if r == 0 and g + 1 < GROUPS:
                     copy_out_stack(g + 1)
             if g + 1 < GROUPS:
                 copy_out_hidden(g + 1)
+            if g == 0:
+                sort_x_group(2, pipeline_runs=True)
+            if g < 2:
+                sort_x_on_scalar(g + 2)
             if g >= 2:
                 sigmoid_group(g - 2)
             if g >= 2:
                 store_group(g - 2)
             if g < GROUPS:
-                mx_product_group(g)
+                for r in range(GROUP_TILES):
+                    mx_product_tile(g, r)
+                    if g == 0 and r == 0:
+                        add_up_biases()
+            if g == 0:
+                for r in range(GROUP_TILES):
+                    add_biases(0, r)
         finish_in_pieces(GROUPS - 1)

@@ -314,7 +314,7 @@ def tile_stackrnn_pa_t_kernel(
         bias_all = consts.tile([P, HDIM], F32)
 
         def add_up_biases():
-            bias_ps = psum_group.tile([P, HDIM], F32, tag="s_t")
+            bias_ps = psum.tile([P, HDIM], F32, tag="mx_ps")
             nc.tensor.matmul(out=bias_ps[:], lhsT=ones[:], rhs=bias_rows[:], start=True, stop=True)
             nc.vector.tensor_copy(out=bias_all[:], in_=bias_ps[:])
 
@@ -347,6 +347,9 @@ def tile_stackrnn_pa_t_kernel(
                 copy_out_hidden(g + 1)
             if g == 0:
                 sort_x_group(2, pipeline_runs=True)
+                add_up_biases()
+                for r in range(GROUP_TILES):
+                    add_biases(g, r)
             if g < 2:
                 sort_x_on_scalar(g + 2)
             if g >= 2:
@@ -356,9 +359,4 @@ def tile_stackrnn_pa_t_kernel(
             if g < GROUPS:
                 for r in range(GROUP_TILES):
                     mx_product_tile(g, r)
-                    if g == 0 and r == 0:
-                        add_up_biases()
-            if g == 0:
-                for r in range(GROUP_TILES):
-                    add_biases(0, r)
         finish_in_pieces(GROUPS - 1)

@@ -28,7 +28,7 @@ GROUP_TILES = 2
 GROUPS = TILES // GROUP_TILES
 OUT_BLOCKS = HDIM // P
 LOAD_AHEAD = 6
-WARM_UP_MATMULS = 4
+WARM_UP_MATMULS = 5
 LAST_PIECE = HDIM // 2
 
 FLOPS = 2 * BATCH * HDIM * (IDIM + HDIM + STACK)
@@ -67,8 +67,12 @@ def tile_stackrnn_pa_t_kernel(
         identity = consts.tile([P, P], F32)
         make_identity(nc, identity[:])
         warm_ps = psum.tile([P, HDIM], F32, tag="mx_ps")
-        for i in range(WARM_UP_MATMULS):
-            nc.tensor.matmul(out=warm_ps[:], lhsT=ones[:], rhs=zeros[:], start=True, stop=True)
+
+        def keep_warm(matmuls=1):
+            for i in range(matmuls):
+                nc.tensor.matmul(out=warm_ps[:], lhsT=ones[:], rhs=zeros[:], start=True, stop=True)
+
+        keep_warm(WARM_UP_MATMULS)
 
         x_in, h_in, s_in = [], [], []
 
@@ -297,20 +301,24 @@ def tile_stackrnn_pa_t_kernel(
         new_group_tiles(0)
         transpose_x(0, 0)
         copy_out_x(0, 0)
+        keep_warm()
         for j in range(OUT_BLOCKS):
             nc.tensor.transpose(w_cat_t[:, j, :], w_cat[:, j, :].bitcast(F32), identity[:])
         nc.vector.tensor_copy(
             out=w_stack[:],
             in_=w_cat_t[:].rearrange("p j n -> p (j n)").bitcast(BF16).rearrange("p (n e) -> p e n", e=2),
         )
+        keep_warm()
         transpose_x(0, 1)
         copy_out_x(0, 1)
         transpose_stack(0)
         copy_out_stack(0)
+        keep_warm()
         for r in range(GROUP_TILES):
             for u in range(HALVES):
                 transpose_hidden(0, r, u)
         copy_out_hidden(0, copy=nc.vector.tensor_copy)
+        keep_warm()
         bias_all = consts.tile([P, HDIM], F32)
 
         def add_up_biases():

from contextlib import ExitStack

import concourse.mybir as mybir
from concourse.masks import make_identity

F32 = mybir.dt.float32
BF16 = mybir.dt.bfloat16
I32 = mybir.dt.int32
U32 = mybir.dt.uint32
U8 = mybir.dt.uint8
FP8X4 = mybir.dt.float8_e4m3fn_x4
FP4X4 = mybir.dt.float4_e2m1fn_x4
ADD = mybir.AluOpType.add
MULT = mybir.AluOpType.mult
SIGMOID = mybir.ActivationFunctionType.Sigmoid

P = 128
PACK = 4
K_PASS = P * PACK
HALVES = 2

BATCH, IDIM, HDIM, STACK = 4096, 1024, 512, 256
X_PASSES = IDIM // K_PASS
H_PASSES = HDIM // K_PASS
W_PASSES = X_PASSES + H_PASSES
TILES = BATCH // P
GROUP_TILES = 2
GROUPS = TILES // GROUP_TILES
OUT_BLOCKS = HDIM // P
LOAD_AHEAD = 6
WARM_UP_MATMULS = 5
LAST_PIECE = HDIM // 2

FLOPS = 2 * BATCH * HDIM * (IDIM + HDIM + STACK)


def tile_stackrnn_pa_t_kernel(
    tc, x, hidden, stack_top, Wi_words, Wi_scales, bi, Wh_words, Wh_scales, bh, W0, b0, W1, b1, out
):
    nc = tc.nc
    x_tiles = x.rearrange("(p t) k -> p t k", t=TILES)
    h_tiles = hidden.rearrange("(p t) k -> p t k", t=TILES)
    s_tiles = stack_top.rearrange("(p t) a s -> p t (a s)", t=TILES)
    out_tiles = out.rearrange("(p t) n -> p t n", t=TILES)

    with ExitStack() as ctx:
        ctx.enter_context(tc.manual_schedule())
        consts = ctx.enter_context(tc.tile_pool(name="consts", bufs=1))
        inputs = ctx.enter_context(tc.tile_pool(name="inputs", bufs=GROUPS))
        work = ctx.enter_context(tc.tile_pool(name="work", bufs=2))
        sorted_pool = ctx.enter_context(tc.tile_pool(name="sorted", bufs=3 * GROUP_TILES))
        results = ctx.enter_context(tc.tile_pool(name="results", bufs=5))
        psum = ctx.enter_context(tc.psum_pool(name="psum", bufs=GROUP_TILES))
        psum_group = ctx.enter_context(tc.psum_pool(name="psum_group", bufs=1))

        ones = consts.tile([P, P], BF16)
        nc.vector.memset(ones[:], 1.0)
        zeros = consts.tile([P, HDIM], BF16)
        nc.vector.memset(zeros[:], 0.0)
        bias_rows = consts.tile([P, HDIM], BF16)
        nc.vector.memset(bias_rows[:], 0.0)
        w_scales = consts.tile([P, W_PASSES, HDIM], U8, align_bytes=64)
        nc.vector.memset(w_scales[:].rearrange("p a n -> p (a n)").bitcast(I32), 0)
        zero_column = consts.tile([P, 1], F32)
        nc.vector.memset(zero_column[:], 0.0)
        port_turn = consts.tile([P, 1], F32)
        identity = consts.tile([P, P], F32)
        make_identity(nc, identity[:])
        warm_ps = psum.tile([P, HDIM], F32, tag="mx_ps")

        def keep_warm(matmuls=1):
            for i in range(matmuls):
                nc.tensor.matmul(out=warm_ps[:], lhsT=ones[:], rhs=zeros[:], start=True, stop=True)

        keep_warm(WARM_UP_MATMULS)

        x_in, h_in, s_in = [], [], []

        def load_group(g, behind_x=None):
            tiles_of_g = slice(g * GROUP_TILES, (g + 1) * GROUP_TILES)
            x_g = inputs.tile([P, GROUP_TILES, IDIM], BF16, name="x_g")
            nc.sync.dma_start(out=x_g[:], in_=x_tiles[:, tiles_of_g, :])
            if behind_x:
                behind_x()
            s_g = inputs.tile([P, GROUP_TILES, STACK], BF16, name="s_g")
            nc.sync.dma_start(out=s_g[:], in_=s_tiles[:, tiles_of_g, :])
            h_g = inputs.tile([P, GROUP_TILES, HDIM], BF16, name="h_g")
            nc.sync.dma_start(out=h_g[:], in_=h_tiles[:, tiles_of_g, :])
            x_in.append(x_g)
            h_in.append(h_g)
            s_in.append(s_g)

        for row, bias in enumerate((bi, bh, b0, b1)):
            nc.gpsimd.dma_start(out=bias_rows[row : row + 1, :], in_=bias.rearrange("(o n) -> o n", o=1))
        w_cat = consts.tile([P, OUT_BLOCKS, STACK], BF16)

        def load_stack_weights():
            nc.sync.dma_start(out=w_cat[:, :, 0 : STACK // 2], in_=W0.rearrange("(j n) s -> n j s", n=P))
            nc.sync.dma_start(out=w_cat[:, :, STACK // 2 : STACK], in_=W1.rearrange("(j n) s -> n j s", n=P))

        w_words = consts.tile([P, W_PASSES, 2 * HDIM], U8, align_bytes=64)

        def load_scales():
            for quadrant in range(4):
                rows = slice(4 * quadrant, 4 * quadrant + 4)
                parts = slice(32 * quadrant, 32 * quadrant + 4)
                nc.sync.dma_start(
                    out=w_scales[parts, 0:X_PASSES, :].bitcast(I32),
                    in_=Wi_scales[:, rows, :].bitcast(I32).rearrange("g r n -> r g n"),
                )
                nc.sync.dma_start(
                    out=w_scales[parts, X_PASSES:W_PASSES, :].bitcast(I32),
                    in_=Wh_scales[:, rows, :].bitcast(I32).rearrange("g r n -> r g n"),
                )

        load_group(0, behind_x=load_stack_weights)
        load_group(1)
        nc.sync.dma_start(
            out=w_words[:, 0:X_PASSES, :].bitcast(I32),
            in_=Wi_words.bitcast(I32).rearrange("g p n -> p g n"),
        )
        nc.sync.dma_start(
            out=w_words[:, X_PASSES:W_PASSES, :].bitcast(I32),
            in_=Wh_words.bitcast(I32).rearrange("g p n -> p g n"),
        )
        load_group(2, behind_x=load_scales)
        for g in range(3, LOAD_AHEAD):
            load_group(g)

        nc.scalar.activation(out=zero_column[:], in_=zero_column[:], func=SIGMOID)

        x_sorted = {}
        x_turned = {}
        h_turned = {}
        s_turned = {}
        grouped = {}
        quantised = {}
        pre_act = {}
        stack_sums = {}
        mx_sums = {}
        words_in_pass = K_PASS // 2

        def sort_x_group(g, pipeline_runs):
            for r in range(GROUP_TILES):
                x_s = sorted_pool.tile([P, X_PASSES, HALVES, P], F32, name="x_sorted")
                x_sorted[(g, r)] = x_s
                words = x_in[g][:, r, :].bitcast(F32).rearrange("p (a c u) -> p a u c", a=X_PASSES, u=HALVES)
                if r == 0:
                    nc.vector.tensor_copy(out=x_s[:, 0], in_=words[:, 0])
                    if not pipeline_runs:
                        nc.scalar.copy(out=x_s[:, 1], in_=words[:, 1])
                elif not pipeline_runs:
                    nc.scalar.copy(out=x_s[:], in_=words)
                else:
                    nc.gpsimd.tensor_copy(out=port_turn[:], in_=x_sorted[(g, 0)][:, 0, 0, 0:1])
                    for a in range(X_PASSES):
                        nc.gpsimd.tensor_scalar(
                            out=x_s[:, a].rearrange("p u c -> p (u c)").bitcast(BF16).rearrange(
                                "p (u c e) -> p u c e", u=HALVES, e=2
                            ),
                            in0=x_in[g][:, r, a * K_PASS : (a + 1) * K_PASS].rearrange(
                                "p (c u e) -> p u c e", u=HALVES, e=2
                            ),
                            scalar1=1.0,
                            scalar2=0.0,
                            op0=MULT,
                            op1=ADD,
                        )

        def sort_x_on_scalar(g):
            words = x_in[g][:, 0, :].bitcast(F32).rearrange("p (a c u) -> p a u c", a=X_PASSES, u=HALVES)
            nc.scalar.copy(out=x_sorted[(g, 0)][:, 1], in_=words[:, 1])

        def transpose_x(g, r):
            x_t = psum.tile([P, X_PASSES, HALVES, P], F32, name="x_t")
            for a in range(X_PASSES):
                for u in range(HALVES):
                    if (g, r) in x_sorted:
                        words = x_sorted[(g, r)][:, a, u, :]
                    else:
                        first = a * words_in_pass + u
                        last = (a + 1) * words_in_pass
                        words = x_in[g][:, r, :].bitcast(F32)[:, first:last:HALVES]
                    nc.tensor.transpose(x_t[:, a, u, :], words, identity[:])
            x_turned[(g, r)] = x_t

        def transpose_stack(g):
            s_words = s_in[g][:].bitcast(F32)
            for r in range(GROUP_TILES):
                nc.tensor.transpose(s_turned[g][:, r, :], s_words[:, r, :], identity[:])

        def transpose_hidden(g, r, u):
            h_words = h_in[g][:].bitcast(F32)
            nc.tensor.transpose(h_turned[g][:, r, u, :], h_words[:, r, u:words_in_pass:HALVES], identity[:])

        def new_group_tiles(g):
            h_turned[g] = psum_group.tile([P, GROUP_TILES, HALVES, P], F32, name="h_t")
            s_turned[g] = psum_group.tile([P, GROUP_TILES, HALVES, P], F32, name="s_t")[:, :, 0, :]
            x_k = work.tile([P, GROUP_TILES, X_PASSES, P, PACK], BF16, name="x_k", align_bytes=64)
            h_k = work.tile([P, GROUP_TILES, P, PACK], BF16, name="h_k", align_bytes=64)
            s_k = work.tile([P, GROUP_TILES, P, 2], BF16, name="s_k")
            grouped[g] = (x_k, h_k, s_k)

        def copy_out_x(g, r):
            x_k = grouped[g][0]
            nc.scalar.copy(
                out=x_k[:, r].rearrange("p a c t -> p a (c t)").bitcast(F32).rearrange("p a (c u) -> p a c u", u=HALVES),
                in_=x_turned[(g, r)][:].rearrange("p a u c -> p a c u"),
            )

        def copy_out_hidden(g, copy=nc.scalar.copy):
            h_k = grouped[g][1]
            copy(
                out=h_k[:].rearrange("p r c t -> p r (c t)").bitcast(F32).rearrange("p r (c u) -> p r c u", u=HALVES),
                in_=h_turned[g][:].rearrange("p r u c -> p r c u"),
            )

        def copy_out_stack(g):
            s_k = grouped[g][2]
            nc.scalar.copy(out=s_k[:].rearrange("p r c e -> p r (c e)").bitcast(F32), in_=s_turned[g])

        def quantise_group(g):
            x_k, h_k, s_k = grouped[g]
            x_codes = work.tile([P, GROUP_TILES, X_PASSES, P], U32, name="x_codes", align_bytes=64)
            x_scales = work.tile([P, GROUP_TILES, X_PASSES, P], U8, name="x_scales", align_bytes=64)
            nc.vector.quantize_mx(
                out=x_codes[:].rearrange("p r a c -> p (r a c)").bitcast(FP8X4),
                scales=x_scales[:].rearrange("p r a c -> p (r a c)"),
                in_=x_k[:].rearrange("p r a c t -> p (r a c t)"),
            )
            h_codes = work.tile([P, GROUP_TILES, P], U32, name="h_codes", align_bytes=64)
            h_scales = work.tile([P, GROUP_TILES, P], U8, name="h_scales", align_bytes=64)
            nc.vector.quantize_mx(
                out=h_codes[:].rearrange("p r c -> p (r c)").bitcast(FP8X4),
                scales=h_scales[:].rearrange("p r c -> p (r c)"),
                in_=h_k[:].rearrange("p r c t -> p (r c t)"),
            )
            quantised[g] = (x_codes, x_scales, h_codes, h_scales)

        def stack_product_tile(g, r, transpose_ahead):
            s_k = grouped[g][2]
            stack_ps = psum.tile([P, HDIM], F32, name="stack_ps")
            nc.tensor.matmul(out=stack_ps[:], lhsT=s_k[:, r, :, 0], rhs=w_stack[:, 0, :], start=True, stop=False)
            if transpose_ahead:
                transpose_hidden(g + 1, r, 0)
                transpose_x(g + 1, r)
            nc.tensor.matmul(out=stack_ps[:], lhsT=s_k[:, r, :, 1], rhs=w_stack[:, 1, :], start=False, stop=True)
            if transpose_ahead:
                transpose_hidden(g + 1, r, 1)
            if transpose_ahead and r == 0:
                transpose_stack(g + 1)
            stack_sums[(g, r)] = stack_ps

        def add_biases(g, r):
            nc.vector.tensor_tensor(out=pre_act[g][:, r, :], in0=stack_sums[(g, r)][:], in1=bias_all[:], op=ADD)

        def mx_product_tile(g, r):
            x_codes, x_scales, h_codes, h_scales = quantised[g]
            mx_ps = psum.tile([P, HDIM], F32, name="mx_ps")
            for a in range(W_PASSES):
                if a < X_PASSES:
                    codes, scales = x_codes[:, r, a, :], x_scales[:, r, a, :]
                else:
                    codes, scales = h_codes[:, r, :], h_scales[:, r, :]
                nc.tensor.matmul_mx(
                    out=mx_ps[:],
                    lhsT=codes.bitcast(FP8X4),
                    lhsT_scale=scales,
                    rhs=w_words[:, a, :].bitcast(FP4X4),
                    rhs_scale=w_scales[:, a, :],
                    start=(a == 0),
                    stop=(a == W_PASSES - 1),
                )
            mx_sums[(g, r)] = mx_ps

        def join_sums_group(g):
            for r in range(GROUP_TILES):
                nc.vector.tensor_tensor(
                    out=pre_act[g][:, r, :], in0=mx_sums[(g, r)][:], in1=pre_act[g][:, r, :], op=ADD
                )

        def sigmoid_group(g):
            sums = pre_act[g][:].rearrange("p r n -> p (r n)")
            nc.scalar.activation(out=sums, in_=sums, func=SIGMOID)

        def store_group(g):
            tiles_of_g = slice(g * GROUP_TILES, (g + 1) * GROUP_TILES)
            nc.sync.dma_start(out=out_tiles[:, tiles_of_g, :], in_=pre_act[g][:])

        def finish_in_pieces(g):
            for r in range(GROUP_TILES):
                for first in range(0, HDIM, LAST_PIECE):
                    cols = slice(first, first + LAST_PIECE)
                    piece = pre_act[g][:, r, cols]
                    nc.vector.tensor_tensor(out=piece, in0=mx_sums[(g, r)][:, cols], in1=piece, op=ADD)
                    nc.scalar.activation(out=piece, in_=piece, func=SIGMOID)
                    nc.sync.dma_start(out=out_tiles[:, g * GROUP_TILES + r, cols], in_=piece)

        w_cat_t = psum.tile([P, OUT_BLOCKS, P], F32, tag="stack_ps")
        w_stack = consts.tile([P, 2, HDIM], BF16)
        new_group_tiles(0)
        transpose_x(0, 0)
        copy_out_x(0, 0)
        keep_warm()
        for j in range(OUT_BLOCKS):
            nc.tensor.transpose(w_cat_t[:, j, :], w_cat[:, j, :].bitcast(F32), identity[:])
        nc.vector.tensor_copy(
            out=w_stack[:],
            in_=w_cat_t[:].rearrange("p j n -> p (j n)").bitcast(BF16).rearrange("p (n e) -> p e n", e=2),
        )
        keep_warm()
        transpose_x(0, 1)
        copy_out_x(0, 1)
        transpose_stack(0)
        copy_out_stack(0)
        keep_warm()
        for r in range(GROUP_TILES):
            for u in range(HALVES):
                transpose_hidden(0, r, u)
        copy_out_hidden(0, copy=nc.vector.tensor_copy)
        keep_warm()
        bias_all = consts.tile([P, HDIM], F32)

        def add_up_biases():
            bias_ps = psum.tile([P, HDIM], F32, tag="mx_ps")
            nc.tensor.matmul(out=bias_ps[:], lhsT=ones[:], rhs=bias_rows[:], start=True, stop=True)
            nc.vector.tensor_copy(out=bias_all[:], in_=bias_ps[:])

        sort_x_group(1, pipeline_runs=False)

        for g in range(GROUPS + 1):
            if g + LOAD_AHEAD < GROUPS:
                load_group(g + LOAD_AHEAD)
            if g < GROUPS:
                quantise_group(g)
                pre_act[g] = results.tile([P, GROUP_TILES, HDIM], F32, name="pre")
            if 1 <= g and g + 2 < GROUPS:
                sort_x_group(g + 2, pipeline_runs=True)
            if 2 <= g and g + 2 < GROUPS:
                sort_x_on_scalar(g + 2)
            if 1 <= g < GROUPS:
                join_sums_group(g - 1)
            if g + 1 < GROUPS:
                new_group_tiles(g + 1)
            for r in range(GROUP_TILES):
                if g < GROUPS:
                    stack_product_tile(g, r, transpose_ahead=(g + 1 < GROUPS))
                if 0 < g < GROUPS:
                    add_biases(g, r)
                if g + 1 < GROUPS:
                    copy_out_x(g + 1, r)
                if r == 0 and g + 1 < GROUPS:
                    copy_out_stack(g + 1)
            if g + 1 < GROUPS:
                copy_out_hidden(g + 1)
            if g == 0:
                sort_x_group(2, pipeline_runs=True)
                add_up_biases()
                for r in range(GROUP_TILES):
                    add_biases(g, r)
            if g < 2:
                sort_x_on_scalar(g + 2)
            if g >= 2:
                sigmoid_group(g - 2)
            if g >= 2:
                store_group(g - 2)
            if g < GROUPS:
                for r in range(GROUP_TILES):
                    mx_product_tile(g, r)
        finish_in_pieces(GROUPS - 1)
